import numpy as np
import ml_dtypes


def mxq(x, axis, fmt="e4m3"):
    dtype, down = {"e4m3": (ml_dtypes.float8_e4m3fn, 7), "e5m2": (ml_dtypes.float8_e5m2, 14)}[fmt]
    v = np.moveaxis(np.asarray(x, np.float32).astype(ml_dtypes.bfloat16).astype(np.float64), axis, -1)
    blocks = v.reshape(v.shape[:-1] + (-1, 32))
    amax = np.abs(blocks).max(-1, keepdims=True)
    byte = np.maximum(np.where(amax > 0, np.frexp(amax)[1] - 1 + 127, 0) - down, 1)
    scale = np.exp2(byte - 127.0)
    codes = (blocks / scale).astype(np.float32).astype(dtype).astype(np.float64)
    return np.moveaxis((codes * scale).reshape(v.shape), -1, axis)


WIDE = False


def mx_kscale(k):
    if not WIDE:
        return np.ones(k)
    levels = np.array([10, -10, 5, -5, 0])
    a = np.random.permutation(np.resize(levels, k // 512 * 4)).reshape(k // 512, 4)
    idx = np.arange(k)
    return np.exp2(a[idx // 512, idx % 128 // 32])


BF16 = ml_dtypes.bfloat16


def bf(x):
    return np.asarray(x, np.float32).astype(BF16)


def f64(x):
    return np.asarray(x).astype(np.float64)


B, IN, HID = 128, 512, 512


def sigmoid(v):
    return 1.0 / (1.0 + np.exp(-v))


def lin(xq, w):
    return xq @ mxq(f64(w), 1, "e4m3").T


def setup_inputs():
    s, p = mx_kscale(IN), mx_kscale(HID)
    return {"inputs": bf(np.random.standard_normal((B, IN)) * s),
            "state": bf(np.random.standard_normal((B, HID))),
            "parent_state": bf(np.random.standard_normal((B, HID)) * p),
            "c": bf(np.tanh(np.random.standard_normal((B, HID)))),
            "w_a_w": bf(np.random.standard_normal((HID, IN)) * 0.6 / np.sqrt(IN) / s),
            "w_a_b": bf(np.random.standard_normal(HID) * 0.5),
            "u_a_w": bf(np.random.standard_normal((HID, HID)) * 0.6 / np.sqrt(HID)),
            "p_a_w": bf(np.random.standard_normal((HID, HID)) * 0.6 / np.sqrt(HID) / p)}


def reference(inputs, state, parent_state, c, w_a_w, w_a_b, u_a_w, p_a_w):
    st = f64(state)
    att = sigmoid(lin(mxq(f64(inputs), 1, "e4m3"), w_a_w) + f64(w_a_b) + lin(mxq(st, 1, "e4m3"), u_a_w) + lin(mxq(f64(parent_state), 1, "e4m3"), p_a_w))
    return att * f64(c) + (1.0 - att) * st

@@ -1,0 +1,177 @@
+from contextlib import ExitStack
+
+import concourse.mybir as mybir
+from concourse.masks import make_identity
+
+F32 = mybir.dt.float32
+BF16 = mybir.dt.bfloat16
+U32 = mybir.dt.uint32
+U8 = mybir.dt.uint8
+FP8X4 = mybir.dt.float8_e4m3fn_x4
+ADD = mybir.AluOpType.add
+SUBTRACT = mybir.AluOpType.subtract
+MULT = mybir.AluOpType.mult
+SIGMOID = mybir.ActivationFunctionType.Sigmoid
+
+P = 128
+K = 512
+HID = 512
+TERMS = 3
+HALVES = 2
+CHUNK = 256
+N_CHUNKS = HID // CHUNK
+ROWS = CHUNK // P
+LOOKAHEAD = 1
+
+FLOPS = 2 * P * K * HID * TERMS
+
+
+def tile_parentgru_pb_s_kernel(
+    tc, inputs, state, parent_state, c, w_a_w, w_a_b, u_a_w, p_a_w, out
+):
+    nc = tc.nc
+    acts = (inputs, state, parent_state)
+    weights = (w_a_w, u_a_w, p_a_w)
+    STATE = 1
+
+    with ExitStack() as ctx:
+        keep = ctx.enter_context(tc.tile_pool(name="keep", bufs=1))
+        work = ctx.enter_context(tc.tile_pool(name="work", bufs=2))
+        psum_t = ctx.enter_context(tc.psum_pool(name="psum_t", bufs=4))
+        psum_acc = ctx.enter_context(tc.psum_pool(name="psum_acc", bufs=2))
+        psum_bias = ctx.enter_context(tc.psum_pool(name="psum_bias", bufs=1))
+        ctx.enter_context(tc.manual_schedule())
+
+        ident = keep.tile([P, P], F32)
+        make_identity(nc, ident[:])
+        bias_row = keep.tile([P, HID], BF16)
+        nc.vector.memset(bias_row[:], 0.0)
+        ones = keep.tile([P, P], BF16)
+        nc.vector.memset(ones[:], 1.0)
+        nc.scalar.dma_start(out=bias_row[0:1, :], in_=w_a_b.rearrange("(o h) -> o h", o=1))
+        warm_in = keep.tile([P, 1], F32)
+        nc.vector.memset(warm_in[:], 0.0)
+        warm_out = keep.tile([P, 1], F32)
+        nc.scalar.activation(out=warm_out[:], in_=warm_in[:], func=SIGMOID)
+
+        x_raw = []
+        for a in range(TERMS):
+            x_tile = keep.tile([P, K], BF16, name="x_raw%d" % a)
+            nc.sync.dma_start(out=x_tile[:], in_=acts[a])
+            x_raw.append(x_tile)
+        c_raw = keep.tile([P, HID], BF16)
+        w_raw = {}
+        for n in range(N_CHUNKS):
+            for a in range(TERMS):
+                w_tile = keep.tile([P, ROWS * K], BF16, name="w_raw%d_%d" % (a, n))
+                nc.sync.dma_start(
+                    out=w_tile[:],
+                    in_=weights[a][n * CHUNK : (n + 1) * CHUNK, :].rearrange(
+                        "(p t) k -> p (t k)", t=ROWS
+                    ),
+                )
+                w_raw[(a, n)] = w_tile
+            if n == 0:
+                nc.sync.dma_start(out=c_raw[:], in_=c)
+
+        x_grouped = keep.tile([P, TERMS * K], BF16, align_bytes=64)
+        x_codes = keep.tile([P, TERMS * P], U32, align_bytes=64)
+        x_scales = keep.tile([P, TERMS * P], U8, align_bytes=64)
+
+        def transpose_rows(bank, b, words):
+            for u in range(HALVES):
+                nc.tensor.transpose(bank[:, b, u, :], words[:, u * P : (u + 1) * P], ident[:])
+
+        bank01 = psum_t.tile([P, 2, HALVES, P], F32, tag="bank")
+        transpose_rows(bank01, 0, x_raw[0][:].bitcast(F32))
+        transpose_rows(bank01, 1, x_raw[1][:].bitcast(F32))
+        nc.scalar.copy(
+            out=x_grouped[:, 0 : 2 * K].bitcast(F32).rearrange("p (b j u) -> p b j u", b=2, u=HALVES),
+            in_=bank01[:].rearrange("p b u j -> p b j u"),
+        )
+        bank2 = psum_t.tile([P, 2, HALVES, P], F32, tag="bank")
+        transpose_rows(bank2, 0, x_raw[2][:].bitcast(F32))
+        nc.vector.tensor_copy(
+            out=x_grouped[:, 2 * K : 3 * K].bitcast(F32).rearrange("p (j u) -> p j u", u=HALVES),
+            in_=bank2[:, 0, :, :].rearrange("p u j -> p j u"),
+        )
+        nc.vector.quantize_mx(
+            out=x_codes[:, 0 : 2 * P].bitcast(FP8X4),
+            scales=x_scales[:, 0 : 2 * P],
+            in_=x_grouped[:, 0 : 2 * K],
+        )
+        nc.vector.quantize_mx(
+            out=x_codes[:, 2 * P : 3 * P].bitcast(FP8X4),
+            scales=x_scales[:, 2 * P : 3 * P],
+            in_=x_grouped[:, 2 * K : 3 * K],
+        )
+
+        bias_ps = psum_bias.tile([P, HID], F32)
+        nc.tensor.matmul(bias_ps[:], lhsT=ones[:], rhs=bias_row[:], start=True, stop=True)
+        bias_sb = keep.tile([P, HID], F32)
+        nc.scalar.copy(out=bias_sb[:], in_=bias_ps[:])
+
+        w_codes = keep.tile([P, TERMS, HID], U32, align_bytes=64)
+        w_scales = keep.tile([P, TERMS, HID], U8, align_bytes=64)
+        diff = keep.tile([P, HID], F32)
+
+        def prepare(a, n):
+            cols = slice(n * CHUNK, (n + 1) * CHUNK)
+            words = w_raw[(a, n)][:].bitcast(F32)
+            bank = psum_t.tile([P, ROWS, HALVES, P], F32, tag="bank")
+            for t in range(ROWS):
+                transpose_rows(bank, t, words[:, t * HALVES * P : (t + 1) * HALVES * P])
+            grouped = work.tile([P, CHUNK * 4], BF16, align_bytes=64, tag="grouped", bufs=3)
+            dst = grouped[:].bitcast(F32).rearrange("p (j t u) -> p j t u", t=ROWS, u=HALVES)
+            src = bank[:].rearrange("p t u j -> p j t u")
+            if a == TERMS - 1 and n == N_CHUNKS - 1:
+                nc.vector.tensor_copy(out=dst, in_=src)
+            else:
+                nc.scalar.copy(out=dst, in_=src)
+            nc.vector.quantize_mx(
+                out=w_codes[:, a, cols].bitcast(FP8X4),
+                scales=w_scales[:, a, cols],
+                in_=grouped[:],
+            )
+
+        gates = {}
+
+        def gate(n):
+            cols = slice(n * CHUNK, (n + 1) * CHUNK)
+            acc = psum_acc.tile([P, CHUNK], F32, tag="acc")
+            for a in range(TERMS):
+                nc.tensor.matmul_mx(
+                    out=acc[:],
+                    lhsT=x_codes[:, a * P : (a + 1) * P].bitcast(FP8X4),
+                    lhsT_scale=x_scales[:, a * P : (a + 1) * P],
+                    rhs=w_codes[:, a, cols].bitcast(FP8X4),
+                    rhs_scale=w_scales[:, a, cols],
+                    start=(a == 0),
+                    stop=(a == TERMS - 1),
+                )
+            logit = work.tile([P, CHUNK], F32, tag="logit")
+            nc.vector.tensor_tensor(out=logit[:], in0=acc[:], in1=bias_sb[:, cols], op=ADD)
+            att = work.tile([P, CHUNK], F32, tag="att")
+            nc.scalar.activation(out=att[:], in_=logit[:], func=SIGMOID)
+            gates[n] = att
+
+        def blend(n):
+            cols = slice(n * CHUNK, (n + 1) * CHUNK)
+            att = gates[n]
+            moved = work.tile([P, CHUNK], F32, tag="moved")
+            nc.vector.tensor_tensor(out=moved[:], in0=att[:], in1=diff[:, cols], op=MULT)
+            result = work.tile([P, CHUNK], F32, tag="result")
+            nc.vector.tensor_tensor(out=result[:], in0=moved[:], in1=x_raw[STATE][:, cols], op=ADD)
+            nc.sync.dma_start(out=out[:, cols], in_=result[:])
+
+        for n in range(N_CHUNKS):
+            for a in range(TERMS):
+                prepare(a, n)
+                if n > 0 and a == LOOKAHEAD:
+                    gate(n - 1)
+            if n == 0:
+                nc.vector.tensor_tensor(out=diff[:], in0=c_raw[:], in1=x_raw[STATE][:], op=SUBTRACT)
+            else:
+                blend(n - 1)
+        gate(N_CHUNKS - 1)
+        blend(N_CHUNKS - 1)

@@ -7,6 +7,7 @@ F32 = mybir.dt.float32
 BF16 = mybir.dt.bfloat16
 U32 = mybir.dt.uint32
 U8 = mybir.dt.uint8
+I32 = mybir.dt.int32
 FP8X4 = mybir.dt.float8_e4m3fn_x4
 ADD = mybir.AluOpType.add
 SUBTRACT = mybir.AluOpType.subtract
@@ -22,6 +23,7 @@ CHUNK = 256
 N_CHUNKS = HID // CHUNK
 ROWS = CHUNK // P
 LOOKAHEAD = 1
+WARM_PASSES = 12
 
 FLOPS = 2 * P * K * HID * TERMS
 
@@ -41,6 +43,23 @@ def tile_parentgru_pb_s_kernel(
         psum_acc = ctx.enter_context(tc.psum_pool(name="psum_acc", bufs=2))
         psum_bias = ctx.enter_context(tc.psum_pool(name="psum_bias", bufs=1))
         ctx.enter_context(tc.manual_schedule())
+
+        zeros = keep.tile([P, 4 * P], BF16, align_bytes=64)
+        nc.vector.memset(zeros[:].bitcast(I32), 0)
+        zero_codes = keep.tile([P, P], U32, align_bytes=64)
+        zero_scales = keep.tile([P, P], U8, align_bytes=64)
+        nc.vector.quantize_mx(out=zero_codes[:].bitcast(FP8X4), scales=zero_scales[:], in_=zeros[:])
+        warm_ps = psum_bias.tile([P, HID], F32, tag="bias")
+        for i in range(WARM_PASSES):
+            nc.tensor.matmul_mx(
+                out=warm_ps[:, 0:P],
+                lhsT=zero_codes[:].bitcast(FP8X4),
+                lhsT_scale=zero_scales[:],
+                rhs=zero_codes[:].bitcast(FP8X4),
+                rhs_scale=zero_scales[:],
+                start=True,
+                stop=True,
+            )
 
         ident = keep.tile([P, P], F32)
         make_identity(nc, ident[:])
@@ -106,7 +125,7 @@ def tile_parentgru_pb_s_kernel(
             in_=x_grouped[:, 2 * K : 3 * K],
         )
 
-        bias_ps = psum_bias.tile([P, HID], F32)
+        bias_ps = psum_bias.tile([P, HID], F32, tag="bias")
         nc.tensor.matmul(bias_ps[:], lhsT=ones[:], rhs=bias_row[:], start=True, stop=True)
         bias_sb = keep.tile([P, HID], F32)
         nc.scalar.copy(out=bias_sb[:], in_=bias_ps[:])

@@ -7,7 +7,6 @@ F32 = mybir.dt.float32
 BF16 = mybir.dt.bfloat16
 U32 = mybir.dt.uint32
 U8 = mybir.dt.uint8
-I32 = mybir.dt.int32
 FP8X4 = mybir.dt.float8_e4m3fn_x4
 ADD = mybir.AluOpType.add
 SUBTRACT = mybir.AluOpType.subtract
@@ -18,12 +17,9 @@ P = 128
 K = 512
 HID = 512
 TERMS = 3
+STATE = 1
 HALVES = 2
-CHUNK = 256
-N_CHUNKS = HID // CHUNK
-ROWS = CHUNK // P
-LOOKAHEAD = 1
-WARM_PASSES = 12
+CHUNK_WIDTHS = (256, 128, 128)
 
 FLOPS = 2 * P * K * HID * TERMS
 
@@ -34,163 +30,118 @@ def tile_parentgru_pb_s_kernel(
     nc = tc.nc
     acts = (inputs, state, parent_state)
     weights = (w_a_w, u_a_w, p_a_w)
-    STATE = 1
+    chunk_cols = []
+    for width in CHUNK_WIDTHS:
+        first = sum(CHUNK_WIDTHS[: len(chunk_cols)])
+        chunk_cols.append(slice(first, first + width))
 
     with ExitStack() as ctx:
         keep = ctx.enter_context(tc.tile_pool(name="keep", bufs=1))
-        work = ctx.enter_context(tc.tile_pool(name="work", bufs=2))
+        work = ctx.enter_context(tc.tile_pool(name="work", bufs=3))
         psum_t = ctx.enter_context(tc.psum_pool(name="psum_t", bufs=4))
-        psum_acc = ctx.enter_context(tc.psum_pool(name="psum_acc", bufs=2))
+        psum_acc = ctx.enter_context(tc.psum_pool(name="psum_acc", bufs=3))
         psum_bias = ctx.enter_context(tc.psum_pool(name="psum_bias", bufs=1))
         ctx.enter_context(tc.manual_schedule())
 
-        zeros = keep.tile([P, 4 * P], BF16, align_bytes=64)
-        nc.vector.memset(zeros[:].bitcast(I32), 0)
-        zero_codes = keep.tile([P, P], U32, align_bytes=64)
-        zero_scales = keep.tile([P, P], U8, align_bytes=64)
-        nc.vector.quantize_mx(out=zero_codes[:].bitcast(FP8X4), scales=zero_scales[:], in_=zeros[:])
-        warm_ps = psum_bias.tile([P, HID], F32, tag="bias")
-        for i in range(WARM_PASSES):
-            nc.tensor.matmul_mx(
-                out=warm_ps[:, 0:P],
-                lhsT=zero_codes[:].bitcast(FP8X4),
-                lhsT_scale=zero_scales[:],
-                rhs=zero_codes[:].bitcast(FP8X4),
-                rhs_scale=zero_scales[:],
-                start=True,
-                stop=True,
-            )
-
-        ident = keep.tile([P, P], F32)
-        make_identity(nc, ident[:])
         bias_row = keep.tile([P, HID], BF16)
         nc.vector.memset(bias_row[:], 0.0)
+        nc.scalar.dma_start(out=bias_row[0:1, :], in_=w_a_b.rearrange("(o h) -> o h", o=1))
         ones = keep.tile([P, P], BF16)
         nc.vector.memset(ones[:], 1.0)
-        nc.scalar.dma_start(out=bias_row[0:1, :], in_=w_a_b.rearrange("(o h) -> o h", o=1))
+        ident = keep.tile([P, P], F32)
+        make_identity(nc, ident[:])
         warm_in = keep.tile([P, 1], F32)
         nc.vector.memset(warm_in[:], 0.0)
         warm_out = keep.tile([P, 1], F32)
         nc.scalar.activation(out=warm_out[:], in_=warm_in[:], func=SIGMOID)
 
-        x_raw = []
-        for a in range(TERMS):
-            x_tile = keep.tile([P, K], BF16, name="x_raw%d" % a)
-            nc.sync.dma_start(out=x_tile[:], in_=acts[a])
-            x_raw.append(x_tile)
+        x_raw = [keep.tile([P, K], BF16, name="x_raw%d" % a) for a in range(TERMS)]
         c_raw = keep.tile([P, HID], BF16)
+        nc.sync.dma_start(out=x_raw[STATE][:], in_=state)
+        nc.sync.dma_start(out=c_raw[:], in_=c)
+        for a in range(TERMS):
+            if a != STATE:
+                nc.sync.dma_start(out=x_raw[a][:], in_=acts[a])
         w_raw = {}
-        for n in range(N_CHUNKS):
+        for n, cols in enumerate(chunk_cols):
+            blocks = CHUNK_WIDTHS[n] // P
             for a in range(TERMS):
-                w_tile = keep.tile([P, ROWS * K], BF16, name="w_raw%d_%d" % (a, n))
+                w_raw[(a, n)] = keep.tile([P, blocks * K], BF16, name="w_raw%d_%d" % (a, n))
                 nc.sync.dma_start(
-                    out=w_tile[:],
-                    in_=weights[a][n * CHUNK : (n + 1) * CHUNK, :].rearrange(
-                        "(p t) k -> p (t k)", t=ROWS
-                    ),
+                    out=w_raw[(a, n)][:],
+                    in_=weights[a][cols, :].rearrange("(p t) k -> p (t k)", t=blocks),
                 )
-                w_raw[(a, n)] = w_tile
-            if n == 0:
-                nc.sync.dma_start(out=c_raw[:], in_=c)
 
-        x_grouped = keep.tile([P, TERMS * K], BF16, align_bytes=64)
-        x_codes = keep.tile([P, TERMS * P], U32, align_bytes=64)
-        x_scales = keep.tile([P, TERMS * P], U8, align_bytes=64)
-
-        def transpose_rows(bank, b, words):
-            for u in range(HALVES):
-                nc.tensor.transpose(bank[:, b, u, :], words[:, u * P : (u + 1) * P], ident[:])
-
-        bank01 = psum_t.tile([P, 2, HALVES, P], F32, tag="bank")
-        transpose_rows(bank01, 0, x_raw[0][:].bitcast(F32))
-        transpose_rows(bank01, 1, x_raw[1][:].bitcast(F32))
-        nc.scalar.copy(
-            out=x_grouped[:, 0 : 2 * K].bitcast(F32).rearrange("p (b j u) -> p b j u", b=2, u=HALVES),
-            in_=bank01[:].rearrange("p b u j -> p b j u"),
-        )
-        bank2 = psum_t.tile([P, 2, HALVES, P], F32, tag="bank")
-        transpose_rows(bank2, 0, x_raw[2][:].bitcast(F32))
-        nc.vector.tensor_copy(
-            out=x_grouped[:, 2 * K : 3 * K].bitcast(F32).rearrange("p (j u) -> p j u", u=HALVES),
-            in_=bank2[:, 0, :, :].rearrange("p u j -> p j u"),
-        )
-        nc.vector.quantize_mx(
-            out=x_codes[:, 0 : 2 * P].bitcast(FP8X4),
-            scales=x_scales[:, 0 : 2 * P],
-            in_=x_grouped[:, 0 : 2 * K],
-        )
-        nc.vector.quantize_mx(
-            out=x_codes[:, 2 * P : 3 * P].bitcast(FP8X4),
-            scales=x_scales[:, 2 * P : 3 * P],
-            in_=x_grouped[:, 2 * K : 3 * K],
-        )
-
-        bias_ps = psum_bias.tile([P, HID], F32, tag="bias")
-        nc.tensor.matmul(bias_ps[:], lhsT=ones[:], rhs=bias_row[:], start=True, stop=True)
-        bias_sb = keep.tile([P, HID], F32)
-        nc.scalar.copy(out=bias_sb[:], in_=bias_ps[:])
-
+        x_codes = keep.tile([P, TERMS, P], U32, align_bytes=64)
+        x_scales = keep.tile([P, TERMS, P], U8, align_bytes=64)
         w_codes = keep.tile([P, TERMS, HID], U32, align_bytes=64)
         w_scales = keep.tile([P, TERMS, HID], U8, align_bytes=64)
-        diff = keep.tile([P, HID], F32)
 
-        def prepare(a, n):
-            cols = slice(n * CHUNK, (n + 1) * CHUNK)
-            words = w_raw[(a, n)][:].bitcast(F32)
-            bank = psum_t.tile([P, ROWS, HALVES, P], F32, tag="bank")
-            for t in range(ROWS):
-                transpose_rows(bank, t, words[:, t * HALVES * P : (t + 1) * HALVES * P])
-            grouped = work.tile([P, CHUNK * 4], BF16, align_bytes=64, tag="grouped", bufs=3)
-            dst = grouped[:].bitcast(F32).rearrange("p (j t u) -> p j t u", t=ROWS, u=HALVES)
-            src = bank[:].rearrange("p t u j -> p j t u")
-            if a == TERMS - 1 and n == N_CHUNKS - 1:
-                nc.vector.tensor_copy(out=dst, in_=src)
-            else:
-                nc.scalar.copy(out=dst, in_=src)
-            nc.vector.quantize_mx(
-                out=w_codes[:, a, cols].bitcast(FP8X4),
-                scales=w_scales[:, a, cols],
-                in_=grouped[:],
+        def transpose_rows(raw, blocks):
+            words = raw[:].bitcast(F32)
+            bank = psum_t.tile([P, blocks, HALVES, P], F32, tag="bank")
+            for t in range(blocks):
+                for u in range(HALVES):
+                    first_word = (t * HALVES + u) * P
+                    nc.tensor.transpose(bank[:, t, u, :], words[:, first_word : first_word + P], ident[:])
+            grouped = work.tile([P, blocks * K], BF16, align_bytes=64, tag="grouped%d" % blocks)
+            nc.scalar.copy(
+                out=grouped[:].bitcast(F32).rearrange("p (j t u) -> p j t u", t=blocks, u=HALVES),
+                in_=bank[:].rearrange("p t u j -> p j t u"),
             )
+            return grouped
 
-        gates = {}
+        def quantise(grouped, codes, scales):
+            nc.vector.quantize_mx(out=codes.bitcast(FP8X4), scales=scales, in_=grouped[:])
 
-        def gate(n):
-            cols = slice(n * CHUNK, (n + 1) * CHUNK)
-            acc = psum_acc.tile([P, CHUNK], F32, tag="acc")
+        diff = keep.tile([P, HID], F32)
+        bias_ps = psum_bias.tile([P, HID], F32)
+        bias_sb = keep.tile([P, HID], F32)
+        waiting = (transpose_rows(x_raw[STATE], 1), x_codes[:, STATE, :], x_scales[:, STATE, :])
+        nc.vector.tensor_tensor(out=diff[:], in0=c_raw[:], in1=x_raw[STATE][:], op=SUBTRACT)
+        nc.tensor.matmul(bias_ps[:], lhsT=ones[:], rhs=bias_row[:], start=True, stop=True)
+        nc.vector.tensor_copy(out=bias_sb[:], in_=bias_ps[:])
+
+        for a in range(TERMS):
+            if a != STATE:
+                grouped = transpose_rows(x_raw[a], 1)
+                quantise(*waiting)
+                waiting = (grouped, x_codes[:, a, :], x_scales[:, a, :])
+        for n, cols in enumerate(chunk_cols):
+            for a in range(TERMS):
+                grouped = transpose_rows(w_raw[(a, n)], CHUNK_WIDTHS[n] // P)
+                quantise(*waiting)
+                waiting = (grouped, w_codes[:, a, cols], w_scales[:, a, cols])
+        quantise(*waiting)
+
+        gates = []
+        for n, cols in enumerate(chunk_cols):
+            width = CHUNK_WIDTHS[n]
+            acc = psum_acc.tile([P, width], F32, tag="acc")
             for a in range(TERMS):
                 nc.tensor.matmul_mx(
                     out=acc[:],
-                    lhsT=x_codes[:, a * P : (a + 1) * P].bitcast(FP8X4),
-                    lhsT_scale=x_scales[:, a * P : (a + 1) * P],
+                    lhsT=x_codes[:, a, :].bitcast(FP8X4),
+                    lhsT_scale=x_scales[:, a, :],
                     rhs=w_codes[:, a, cols].bitcast(FP8X4),
                     rhs_scale=w_scales[:, a, cols],
                     start=(a == 0),
                     stop=(a == TERMS - 1),
                 )
-            logit = work.tile([P, CHUNK], F32, tag="logit")
+            logit = work.tile([P, width], F32, tag="logit")
             nc.vector.tensor_tensor(out=logit[:], in0=acc[:], in1=bias_sb[:, cols], op=ADD)
-            att = work.tile([P, CHUNK], F32, tag="att")
+            att = work.tile([P, width], F32, tag="att")
             nc.scalar.activation(out=att[:], in_=logit[:], func=SIGMOID)
-            gates[n] = att
+            gates.append(att)
 
-        def blend(n):
-            cols = slice(n * CHUNK, (n + 1) * CHUNK)
-            att = gates[n]
-            moved = work.tile([P, CHUNK], F32, tag="moved")
-            nc.vector.tensor_tensor(out=moved[:], in0=att[:], in1=diff[:, cols], op=MULT)
-            result = work.tile([P, CHUNK], F32, tag="result")
-            nc.vector.tensor_tensor(out=result[:], in0=moved[:], in1=x_raw[STATE][:, cols], op=ADD)
-            nc.sync.dma_start(out=out[:, cols], in_=result[:])
-
-        for n in range(N_CHUNKS):
-            for a in range(TERMS):
-                prepare(a, n)
-                if n > 0 and a == LOOKAHEAD:
-                    gate(n - 1)
-            if n == 0:
-                nc.vector.tensor_tensor(out=diff[:], in0=c_raw[:], in1=x_raw[STATE][:], op=SUBTRACT)
-            else:
-                blend(n - 1)
-        gate(N_CHUNKS - 1)
-        blend(N_CHUNKS - 1)
+        moved = []
+        for n in range(len(chunk_cols) + 1):
+            if n < len(chunk_cols):
+                product = work.tile([P, CHUNK_WIDTHS[n]], F32, tag="moved")
+                nc.vector.tensor_tensor(out=product[:], in0=gates[n][:], in1=diff[:, chunk_cols[n]], op=MULT)
+                moved.append(product)
+            if n > 0:
+                cols = chunk_cols[n - 1]
+                result = work.tile([P, CHUNK_WIDTHS[n - 1]], F32, tag="result")
+                nc.vector.tensor_tensor(out=result[:], in0=moved[n - 1][:], in1=x_raw[STATE][:, cols], op=ADD)
+                nc.sync.dma_start(out=out[:, cols], in_=result[:])

@@ -19,7 +19,6 @@ HID = 512
 TERMS = 3
 STATE = 1
 HALVES = 2
-CHUNK_WIDTHS = (256, 128, 128)
 
 FLOPS = 2 * P * K * HID * TERMS
 
@@ -30,10 +29,7 @@ def tile_parentgru_pb_s_kernel(
     nc = tc.nc
     acts = (inputs, state, parent_state)
     weights = (w_a_w, u_a_w, p_a_w)
-    chunk_cols = []
-    for width in CHUNK_WIDTHS:
-        first = sum(CHUNK_WIDTHS[: len(chunk_cols)])
-        chunk_cols.append(slice(first, first + width))
+    chunk_cols = (slice(0, 256), slice(256, 384), slice(384, 512))
 
     with ExitStack() as ctx:
         keep = ctx.enter_context(tc.tile_pool(name="keep", bufs=1))
@@ -43,17 +39,16 @@ def tile_parentgru_pb_s_kernel(
         psum_bias = ctx.enter_context(tc.psum_pool(name="psum_bias", bufs=1))
         ctx.enter_context(tc.manual_schedule())
 
-        bias_row = keep.tile([P, HID], BF16)
-        nc.vector.memset(bias_row[:], 0.0)
-        nc.scalar.dma_start(out=bias_row[0:1, :], in_=w_a_b.rearrange("(o h) -> o h", o=1))
-        ones = keep.tile([P, P], BF16)
-        nc.vector.memset(ones[:], 1.0)
         ident = keep.tile([P, P], F32)
         make_identity(nc, ident[:])
         warm_in = keep.tile([P, 1], F32)
         nc.vector.memset(warm_in[:], 0.0)
         warm_out = keep.tile([P, 1], F32)
         nc.scalar.activation(out=warm_out[:], in_=warm_in[:], func=SIGMOID)
+        bias_row = keep.tile([P, HID], BF16)
+        nc.vector.memset(bias_row[:], 0.0)
+        ones = keep.tile([P, P], BF16)
+        nc.vector.memset(ones[:], 1.0)
 
         x_raw = [keep.tile([P, K], BF16, name="x_raw%d" % a) for a in range(TERMS)]
         c_raw = keep.tile([P, HID], BF16)
@@ -62,22 +57,23 @@ def tile_parentgru_pb_s_kernel(
         for a in range(TERMS):
             if a != STATE:
                 nc.sync.dma_start(out=x_raw[a][:], in_=acts[a])
+        nc.sync.dma_start(out=bias_row[0:1, :], in_=w_a_b.rearrange("(o h) -> o h", o=1))
+        w_loads = [(0, 0, 2), (1, 0, 2), (2, 0, 2), (0, 256, 2), (1, 256, 2), (2, 256, 1), (2, 384, 1)]
         w_raw = {}
-        for n, cols in enumerate(chunk_cols):
-            blocks = CHUNK_WIDTHS[n] // P
-            for a in range(TERMS):
-                w_raw[(a, n)] = keep.tile([P, blocks * K], BF16, name="w_raw%d_%d" % (a, n))
-                nc.sync.dma_start(
-                    out=w_raw[(a, n)][:],
-                    in_=weights[a][cols, :].rearrange("(p t) k -> p (t k)", t=blocks),
-                )
+        for a, first, blocks in w_loads:
+            raw = keep.tile([P, blocks * K], BF16, name="w_raw%d_%d" % (a, first))
+            nc.sync.dma_start(
+                out=raw[:],
+                in_=weights[a][first : first + blocks * P, :].rearrange("(p t) k -> p (t k)", t=blocks),
+            )
+            w_raw[(a, first)] = raw
 
         x_codes = keep.tile([P, TERMS, P], U32, align_bytes=64)
         x_scales = keep.tile([P, TERMS, P], U8, align_bytes=64)
         w_codes = keep.tile([P, TERMS, HID], U32, align_bytes=64)
         w_scales = keep.tile([P, TERMS, HID], U8, align_bytes=64)
 
-        def transpose_rows(raw, blocks):
+        def transpose_rows(raw, blocks, copy):
             words = raw[:].bitcast(F32)
             bank = psum_t.tile([P, blocks, HALVES, P], F32, tag="bank")
             for t in range(blocks):
@@ -85,7 +81,7 @@ def tile_parentgru_pb_s_kernel(
                     first_word = (t * HALVES + u) * P
                     nc.tensor.transpose(bank[:, t, u, :], words[:, first_word : first_word + P], ident[:])
             grouped = work.tile([P, blocks * K], BF16, align_bytes=64, tag="grouped%d" % blocks)
-            nc.scalar.copy(
+            copy(
                 out=grouped[:].bitcast(F32).rearrange("p (j t u) -> p j t u", t=blocks, u=HALVES),
                 in_=bank[:].rearrange("p t u j -> p j t u"),
             )
@@ -97,26 +93,8 @@ def tile_parentgru_pb_s_kernel(
         diff = keep.tile([P, HID], F32)
         bias_ps = psum_bias.tile([P, HID], F32)
         bias_sb = keep.tile([P, HID], F32)
-        waiting = (transpose_rows(x_raw[STATE], 1), x_codes[:, STATE, :], x_scales[:, STATE, :])
-        nc.vector.tensor_tensor(out=diff[:], in0=c_raw[:], in1=x_raw[STATE][:], op=SUBTRACT)
-        nc.tensor.matmul(bias_ps[:], lhsT=ones[:], rhs=bias_row[:], start=True, stop=True)
-        nc.vector.tensor_copy(out=bias_sb[:], in_=bias_ps[:])
 
-        for a in range(TERMS):
-            if a != STATE:
-                grouped = transpose_rows(x_raw[a], 1)
-                quantise(*waiting)
-                waiting = (grouped, x_codes[:, a, :], x_scales[:, a, :])
-        for n, cols in enumerate(chunk_cols):
-            for a in range(TERMS):
-                grouped = transpose_rows(w_raw[(a, n)], CHUNK_WIDTHS[n] // P)
-                quantise(*waiting)
-                waiting = (grouped, w_codes[:, a, cols], w_scales[:, a, cols])
-        quantise(*waiting)
-
-        gates = []
-        for n, cols in enumerate(chunk_cols):
-            width = CHUNK_WIDTHS[n]
+        def accumulate(cols, width):
             acc = psum_acc.tile([P, width], F32, tag="acc")
             for a in range(TERMS):
                 nc.tensor.matmul_mx(
@@ -128,20 +106,65 @@ def tile_parentgru_pb_s_kernel(
                     start=(a == 0),
                     stop=(a == TERMS - 1),
                 )
+            return acc
+
+        def gate(acc, cols, width):
             logit = work.tile([P, width], F32, tag="logit")
             nc.vector.tensor_tensor(out=logit[:], in0=acc[:], in1=bias_sb[:, cols], op=ADD)
             att = work.tile([P, width], F32, tag="att")
             nc.scalar.activation(out=att[:], in_=logit[:], func=SIGMOID)
-            gates.append(att)
+            return att
 
-        moved = []
-        for n in range(len(chunk_cols) + 1):
-            if n < len(chunk_cols):
-                product = work.tile([P, CHUNK_WIDTHS[n]], F32, tag="moved")
-                nc.vector.tensor_tensor(out=product[:], in0=gates[n][:], in1=diff[:, chunk_cols[n]], op=MULT)
-                moved.append(product)
-            if n > 0:
-                cols = chunk_cols[n - 1]
-                result = work.tile([P, CHUNK_WIDTHS[n - 1]], F32, tag="result")
-                nc.vector.tensor_tensor(out=result[:], in0=moved[n - 1][:], in1=x_raw[STATE][:, cols], op=ADD)
-                nc.sync.dma_start(out=out[:, cols], in_=result[:])
+        def scale_by_diff(att, cols, width):
+            product = work.tile([P, width], F32, tag="moved")
+            nc.vector.tensor_tensor(out=product[:], in0=att[:], in1=diff[:, cols], op=MULT)
+            return product
+
+        def finish(product, cols, width):
+            result = work.tile([P, width], F32, tag="result")
+            nc.vector.tensor_tensor(out=result[:], in0=product[:], in1=x_raw[STATE][:, cols], op=ADD)
+            nc.sync.dma_start(out=out[:, cols], in_=result[:])
+
+        SC, VC = nc.scalar.copy, nc.vector.tensor_copy
+
+        pending = []
+
+        def stage(raw, blocks, copy, codes, scales):
+            grouped = transpose_rows(raw, blocks, copy)
+            if pending:
+                quantise(*pending.pop())
+            pending.append((grouped, codes, scales))
+
+        def stage_x(a, copy):
+            stage(x_raw[a], 1, copy, x_codes[:, a, :], x_scales[:, a, :])
+
+        def stage_w(a, first, blocks, copy):
+            cols = slice(first, first + blocks * P)
+            stage(w_raw[(a, first)], blocks, copy, w_codes[:, a, cols], w_scales[:, a, cols])
+
+        stage_x(STATE, SC)
+        nc.vector.tensor_tensor(out=diff[:], in0=c_raw[:], in1=x_raw[STATE][:], op=SUBTRACT)
+        stage_x(0, SC)
+        stage_x(2, VC)
+        stage_w(0, 0, 2, VC)
+        stage_w(1, 0, 2, SC)
+        stage_w(2, 0, 2, SC)
+        stage_w(0, 256, 2, VC)
+        nc.tensor.matmul(bias_ps[:], lhsT=ones[:], rhs=bias_row[:], start=True, stop=True)
+        nc.scalar.copy(out=bias_sb[:], in_=bias_ps[:])
+        acc0 = accumulate(chunk_cols[0], 256)
+        stage_w(1, 256, 2, SC)
+        att0 = gate(acc0, chunk_cols[0], 256)
+        stage_w(2, 256, 1, VC)
+        product0 = scale_by_diff(att0, chunk_cols[0], 256)
+        stage_w(2, 384, 1, SC)
+        finish(product0, chunk_cols[0], 256)
+        quantise(*pending.pop())
+        acc1 = accumulate(chunk_cols[1], P)
+        acc2 = accumulate(chunk_cols[2], P)
+        att1 = gate(acc1, chunk_cols[1], P)
+        att2 = gate(acc2, chunk_cols[2], P)
+        product1 = scale_by_diff(att1, chunk_cols[1], P)
+        product2 = scale_by_diff(att2, chunk_cols[2], P)
+        finish(product1, chunk_cols[1], P)
+        finish(product2, chunk_cols[2], P)

@@ -18,6 +18,7 @@ K = 512
 HID = 512
 TERMS = 3
 STATE = 1
+WARM_UPS = 12
 HALVES = 2
 
 FLOPS = 2 * P * K * HID * TERMS
@@ -142,29 +143,31 @@ def tile_parentgru_pb_s_kernel(
             cols = slice(first, first + blocks * P)
             stage(w_raw[(a, first)], blocks, copy, w_codes[:, a, cols], w_scales[:, a, cols])
 
+        for i in range(WARM_UPS):
+            nc.tensor.transpose(bias_ps[:, 0:P], ident[:], ident[:])
         stage_x(STATE, SC)
         nc.vector.tensor_tensor(out=diff[:], in0=c_raw[:], in1=x_raw[STATE][:], op=SUBTRACT)
         stage_x(0, SC)
         stage_x(2, VC)
         stage_w(0, 0, 2, VC)
+        nc.tensor.matmul(bias_ps[:], lhsT=ones[:], rhs=bias_row[:], start=True, stop=True)
+        nc.scalar.copy(out=bias_sb[:], in_=bias_ps[:])
         stage_w(1, 0, 2, SC)
         stage_w(2, 0, 2, SC)
         stage_w(0, 256, 2, VC)
-        nc.tensor.matmul(bias_ps[:], lhsT=ones[:], rhs=bias_row[:], start=True, stop=True)
-        nc.scalar.copy(out=bias_sb[:], in_=bias_ps[:])
-        acc0 = accumulate(chunk_cols[0], 256)
         stage_w(1, 256, 2, SC)
-        att0 = gate(acc0, chunk_cols[0], 256)
         stage_w(2, 256, 1, VC)
-        product0 = scale_by_diff(att0, chunk_cols[0], 256)
         stage_w(2, 384, 1, SC)
-        finish(product0, chunk_cols[0], 256)
+        acc0 = accumulate(chunk_cols[0], 256)
+        att0 = gate(acc0, chunk_cols[0], 256)
         quantise(*pending.pop())
         acc1 = accumulate(chunk_cols[1], P)
         acc2 = accumulate(chunk_cols[2], P)
         att1 = gate(acc1, chunk_cols[1], P)
         att2 = gate(acc2, chunk_cols[2], P)
+        product0 = scale_by_diff(att0, chunk_cols[0], 256)
         product1 = scale_by_diff(att1, chunk_cols[1], P)
+        finish(product0, chunk_cols[0], 256)
         product2 = scale_by_diff(att2, chunk_cols[2], P)
         finish(product1, chunk_cols[1], P)
         finish(product2, chunk_cols[2], P)

@@ -16,10 +16,11 @@ SIGMOID = mybir.ActivationFunctionType.Sigmoid
 P = 128
 K = 512
 HID = 512
+BLOCKS = HID // P
 TERMS = 3
 STATE = 1
-WARM_UPS = 12
 HALVES = 2
+WARM_UPS = 12
 
 FLOPS = 2 * P * K * HID * TERMS
 
@@ -30,11 +31,11 @@ def tile_parentgru_pb_s_kernel(
     nc = tc.nc
     acts = (inputs, state, parent_state)
     weights = (w_a_w, u_a_w, p_a_w)
-    chunk_cols = (slice(0, 256), slice(256, 384), slice(384, 512))
+    SC, VC = nc.scalar.copy, nc.vector.tensor_copy
 
     with ExitStack() as ctx:
         keep = ctx.enter_context(tc.tile_pool(name="keep", bufs=1))
-        work = ctx.enter_context(tc.tile_pool(name="work", bufs=3))
+        work = ctx.enter_context(tc.tile_pool(name="work", bufs=4))
         psum_t = ctx.enter_context(tc.psum_pool(name="psum_t", bufs=4))
         psum_acc = ctx.enter_context(tc.psum_pool(name="psum_acc", bufs=3))
         psum_bias = ctx.enter_context(tc.psum_pool(name="psum_bias", bufs=1))
@@ -48,26 +49,36 @@ def tile_parentgru_pb_s_kernel(
         nc.scalar.activation(out=warm_out[:], in_=warm_in[:], func=SIGMOID)
         bias_row = keep.tile([P, HID], BF16)
         nc.vector.memset(bias_row[:], 0.0)
-        ones = keep.tile([P, P], BF16)
+        ones = keep.tile([P, 1], BF16)
         nc.vector.memset(ones[:], 1.0)
 
         x_raw = [keep.tile([P, K], BF16, name="x_raw%d" % a) for a in range(TERMS)]
         c_raw = keep.tile([P, HID], BF16)
-        nc.sync.dma_start(out=x_raw[STATE][:], in_=state)
-        nc.sync.dma_start(out=c_raw[:], in_=c)
-        for a in range(TERMS):
-            if a != STATE:
-                nc.sync.dma_start(out=x_raw[a][:], in_=acts[a])
-        nc.sync.dma_start(out=bias_row[0:1, :], in_=w_a_b.rearrange("(o h) -> o h", o=1))
-        w_loads = [(0, 0, 2), (1, 0, 2), (2, 0, 2), (0, 256, 2), (1, 256, 2), (2, 256, 1), (2, 384, 1)]
         w_raw = {}
-        for a, first, blocks in w_loads:
+
+        def load_x(a):
+            nc.sync.dma_start(out=x_raw[a][:], in_=acts[a])
+
+        def load_w(a, first, blocks):
             raw = keep.tile([P, blocks * K], BF16, name="w_raw%d_%d" % (a, first))
             nc.sync.dma_start(
                 out=raw[:],
                 in_=weights[a][first : first + blocks * P, :].rearrange("(p t) k -> p (t k)", t=blocks),
             )
             w_raw[(a, first)] = raw
+
+        load_x(STATE)
+        load_w(0, 0, 2)
+        load_w(1, 0, 2)
+        nc.sync.dma_start(out=bias_row[0:1, :], in_=w_a_b.rearrange("(o h) -> o h", o=1))
+        load_x(0)
+        load_x(2)
+        load_w(2, 0, 2)
+        nc.sync.dma_start(out=c_raw[:], in_=c)
+        load_w(0, 256, 2)
+        load_w(1, 256, 2)
+        load_w(2, 256, 1)
+        load_w(2, 384, 1)
 
         x_codes = keep.tile([P, TERMS, P], U32, align_bytes=64)
         x_scales = keep.tile([P, TERMS, P], U8, align_bytes=64)
@@ -91,43 +102,6 @@ def tile_parentgru_pb_s_kernel(
         def quantise(grouped, codes, scales):
             nc.vector.quantize_mx(out=codes.bitcast(FP8X4), scales=scales, in_=grouped[:])
 
-        diff = keep.tile([P, HID], F32)
-        bias_ps = psum_bias.tile([P, HID], F32)
-        bias_sb = keep.tile([P, HID], F32)
-
-        def accumulate(cols, width):
-            acc = psum_acc.tile([P, width], F32, tag="acc")
-            for a in range(TERMS):
-                nc.tensor.matmul_mx(
-                    out=acc[:],
-                    lhsT=x_codes[:, a, :].bitcast(FP8X4),
-                    lhsT_scale=x_scales[:, a, :],
-                    rhs=w_codes[:, a, cols].bitcast(FP8X4),
-                    rhs_scale=w_scales[:, a, cols],
-                    start=(a == 0),
-                    stop=(a == TERMS - 1),
-                )
-            return acc
-
-        def gate(acc, cols, width):
-            logit = work.tile([P, width], F32, tag="logit")
-            nc.vector.tensor_tensor(out=logit[:], in0=acc[:], in1=bias_sb[:, cols], op=ADD)
-            att = work.tile([P, width], F32, tag="att")
-            nc.scalar.activation(out=att[:], in_=logit[:], func=SIGMOID)
-            return att
-
-        def scale_by_diff(att, cols, width):
-            product = work.tile([P, width], F32, tag="moved")
-            nc.vector.tensor_tensor(out=product[:], in0=att[:], in1=diff[:, cols], op=MULT)
-            return product
-
-        def finish(product, cols, width):
-            result = work.tile([P, width], F32, tag="result")
-            nc.vector.tensor_tensor(out=result[:], in0=product[:], in1=x_raw[STATE][:, cols], op=ADD)
-            nc.sync.dma_start(out=out[:, cols], in_=result[:])
-
-        SC, VC = nc.scalar.copy, nc.vector.tensor_copy
-
         pending = []
 
         def stage(raw, blocks, copy, codes, scales):
@@ -143,31 +117,75 @@ def tile_parentgru_pb_s_kernel(
             cols = slice(first, first + blocks * P)
             stage(w_raw[(a, first)], blocks, copy, w_codes[:, a, cols], w_scales[:, a, cols])
 
+        def gate(block):
+            cols = slice(block * P, (block + 1) * P)
+            acc = psum_acc.tile([P, P], F32, tag="acc")
+            for a in range(TERMS):
+                nc.tensor.matmul_mx(
+                    out=acc[:],
+                    lhsT=w_codes[:, a, cols].bitcast(FP8X4),
+                    lhsT_scale=w_scales[:, a, cols],
+                    rhs=x_codes[:, a, :].bitcast(FP8X4),
+                    rhs_scale=x_scales[:, a, :],
+                    start=(a == 0),
+                    stop=(a == TERMS - 1),
+                )
+            att = work.tile([P, P], F32, tag="att")
+            nc.scalar.activation(out=att[:], in_=acc[:], func=SIGMOID, bias=bias_col[:, block : block + 1])
+            return att
+
+        def turn(atts):
+            bank = psum_t.tile([P, len(atts), P], F32, tag="bank")
+            for i, att in enumerate(atts):
+                nc.tensor.transpose(bank[:, i, :], att[:], ident[:])
+            return bank
+
+        def scale_by_diff(bank, cols, width):
+            product = work.tile([P, width], F32, tag="moved")
+            nc.vector.tensor_tensor(
+                out=product[:], in0=bank[:].rearrange("p i h -> p (i h)"), in1=diff[:, cols], op=MULT
+            )
+            return product
+
+        def finish(product, cols, width):
+            result = work.tile([P, width], F32, tag="result")
+            nc.vector.tensor_tensor(out=result[:], in0=product[:], in1=x_raw[STATE][:, cols], op=ADD)
+            nc.sync.dma_start(out=out[:, cols], in_=result[:])
+
+        cols_a, cols_b, cols_c = slice(0, 256), slice(256, 384), slice(384, 512)
+        diff = keep.tile([P, HID], F32)
+        bias_ps = psum_bias.tile([P, HID], F32)
+        bias_col = keep.tile([P, BLOCKS], F32)
+
         for i in range(WARM_UPS):
-            nc.tensor.transpose(bias_ps[:, 0:P], ident[:], ident[:])
-        stage_x(STATE, SC)
-        nc.vector.tensor_tensor(out=diff[:], in0=c_raw[:], in1=x_raw[STATE][:], op=SUBTRACT)
+            nc.tensor.transpose(bias_ps[:, P : 2 * P], ident[:], ident[:])
+        stage_x(STATE, VC)
+        stage_w(0, 0, 2, SC)
+        stage_w(1, 0, 2, VC)
+        for j in range(BLOCKS):
+            nc.tensor.matmul(
+                bias_ps[:, j : j + 1], lhsT=bias_row[:, j * P : (j + 1) * P], rhs=ones[:], start=True, stop=True
+            )
         stage_x(0, SC)
-        stage_x(2, VC)
-        stage_w(0, 0, 2, VC)
-        nc.tensor.matmul(bias_ps[:], lhsT=ones[:], rhs=bias_row[:], start=True, stop=True)
-        nc.scalar.copy(out=bias_sb[:], in_=bias_ps[:])
-        stage_w(1, 0, 2, SC)
+        nc.scalar.copy(out=bias_col[:], in_=bias_ps[:, 0:BLOCKS])
+        stage_x(2, SC)
         stage_w(2, 0, 2, SC)
-        stage_w(0, 256, 2, VC)
+        nc.vector.tensor_tensor(out=diff[:], in0=c_raw[:], in1=x_raw[STATE][:], op=SUBTRACT)
+        stage_w(0, 256, 2, SC)
         stage_w(1, 256, 2, SC)
         stage_w(2, 256, 1, VC)
         stage_w(2, 384, 1, SC)
-        acc0 = accumulate(chunk_cols[0], 256)
-        att0 = gate(acc0, chunk_cols[0], 256)
+        att_0 = gate(0)
+        att_1 = gate(1)
         quantise(*pending.pop())
-        acc1 = accumulate(chunk_cols[1], P)
-        acc2 = accumulate(chunk_cols[2], P)
-        att1 = gate(acc1, chunk_cols[1], P)
-        att2 = gate(acc2, chunk_cols[2], P)
-        product0 = scale_by_diff(att0, chunk_cols[0], 256)
-        product1 = scale_by_diff(att1, chunk_cols[1], P)
-        finish(product0, chunk_cols[0], 256)
-        product2 = scale_by_diff(att2, chunk_cols[2], P)
-        finish(product1, chunk_cols[1], P)
-        finish(product2, chunk_cols[2], P)
+        att_2 = gate(2)
+        att_3 = gate(3)
+        turned_a = turn((att_0, att_1))
+        product_a = scale_by_diff(turned_a, cols_a, 256)
+        turned_b = turn((att_2,))
+        turned_c = turn((att_3,))
+        finish(product_a, cols_a, 256)
+        product_b = scale_by_diff(turned_b, cols_b, P)
+        product_c = scale_by_diff(turned_c, cols_c, P)
+        finish(product_b, cols_b, P)
+        finish(product_c, cols_c, P)

@@ -20,7 +20,7 @@ BLOCKS = HID // P
 TERMS = 3
 STATE = 1
 HALVES = 2
-WARM_UPS = 12
+WARM_UPS = 3
 
 FLOPS = 2 * P * K * HID * TERMS
 
@@ -152,16 +152,21 @@ def tile_parentgru_pb_s_kernel(
             nc.vector.tensor_tensor(out=result[:], in0=product[:], in1=x_raw[STATE][:, cols], op=ADD)
             nc.sync.dma_start(out=out[:, cols], in_=result[:])
 
+        def busy(width):
+            nc.tensor.matmul(bias_ps[:, P : P + width], lhsT=ident[:], rhs=ident[:, 0:width], start=True, stop=True)
+
         cols_a, cols_b, cols_c = slice(0, 256), slice(256, 384), slice(384, 512)
         diff = keep.tile([P, HID], F32)
         bias_ps = psum_bias.tile([P, HID], F32)
         bias_col = keep.tile([P, BLOCKS], F32)
 
         for i in range(WARM_UPS):
-            nc.tensor.transpose(bias_ps[:, P : 2 * P], ident[:], ident[:])
+            busy(P)
         stage_x(STATE, VC)
         stage_w(0, 0, 2, SC)
+        busy(32)
         stage_w(1, 0, 2, VC)
+        busy(32)
         for j in range(BLOCKS):
             nc.tensor.matmul(
                 bias_ps[:, j : j + 1], lhsT=bias_row[:, j * P : (j + 1) * P], rhs=ones[:], start=True, stop=True
@@ -169,10 +174,14 @@ def tile_parentgru_pb_s_kernel(
         stage_x(0, SC)
         nc.scalar.copy(out=bias_col[:], in_=bias_ps[:, 0:BLOCKS])
         stage_x(2, SC)
+        busy(32)
         stage_w(2, 0, 2, SC)
+        busy(32)
         nc.vector.tensor_tensor(out=diff[:], in0=c_raw[:], in1=x_raw[STATE][:], op=SUBTRACT)
         stage_w(0, 256, 2, SC)
+        busy(32)
         stage_w(1, 256, 2, SC)
+        busy(32)
         stage_w(2, 256, 1, VC)
         stage_w(2, 384, 1, SC)
         att_0 = gate(0)

@@ -20,7 +20,7 @@ BLOCKS = HID // P
 TERMS = 3
 STATE = 1
 HALVES = 2
-WARM_UPS = 3
+WARM_UPS = 4
 
 FLOPS = 2 * P * K * HID * TERMS
 
@@ -37,10 +37,13 @@ def tile_parentgru_pb_s_kernel(
         keep = ctx.enter_context(tc.tile_pool(name="keep", bufs=1))
         work = ctx.enter_context(tc.tile_pool(name="work", bufs=4))
         psum_t = ctx.enter_context(tc.psum_pool(name="psum_t", bufs=4))
-        psum_acc = ctx.enter_context(tc.psum_pool(name="psum_acc", bufs=3))
+        psum_acc = ctx.enter_context(tc.psum_pool(name="psum_acc", bufs=2))
+        psum_idle = ctx.enter_context(tc.psum_pool(name="psum_idle", bufs=1))
         psum_bias = ctx.enter_context(tc.psum_pool(name="psum_bias", bufs=1))
         ctx.enter_context(tc.manual_schedule())
 
+        warm_src = keep.tile([P, P], F32)
+        nc.vector.memset(warm_src[:], 1.0)
         ident = keep.tile([P, P], F32)
         make_identity(nc, ident[:])
         warm_in = keep.tile([P, 1], F32)
@@ -153,20 +156,23 @@ def tile_parentgru_pb_s_kernel(
             nc.sync.dma_start(out=out[:, cols], in_=result[:])
 
         def busy(width):
-            nc.tensor.matmul(bias_ps[:, P : P + width], lhsT=ident[:], rhs=ident[:, 0:width], start=True, stop=True)
+            nc.tensor.matmul(idle_ps[:, 0:width], lhsT=warm_src[:], rhs=warm_src[:, 0:width], start=True, stop=True)
 
         cols_a, cols_b, cols_c = slice(0, 256), slice(256, 384), slice(384, 512)
         diff = keep.tile([P, HID], F32)
         bias_ps = psum_bias.tile([P, HID], F32)
+        idle_ps = psum_idle.tile([P, P], F32)
         bias_col = keep.tile([P, BLOCKS], F32)
 
         for i in range(WARM_UPS):
             busy(P)
+        for i in range(4):
+            nc.tensor.transpose(idle_ps[:], ident[:], ident[:])
         stage_x(STATE, VC)
         stage_w(0, 0, 2, SC)
-        busy(32)
+        busy(16)
         stage_w(1, 0, 2, VC)
-        busy(32)
+        busy(16)
         for j in range(BLOCKS):
             nc.tensor.matmul(
                 bias_ps[:, j : j + 1], lhsT=bias_row[:, j * P : (j + 1) * P], rhs=ones[:], start=True, stop=True
@@ -174,14 +180,14 @@ def tile_parentgru_pb_s_kernel(
         stage_x(0, SC)
         nc.scalar.copy(out=bias_col[:], in_=bias_ps[:, 0:BLOCKS])
         stage_x(2, SC)
-        busy(32)
+        busy(16)
         stage_w(2, 0, 2, SC)
-        busy(32)
+        busy(16)
         nc.vector.tensor_tensor(out=diff[:], in0=c_raw[:], in1=x_raw[STATE][:], op=SUBTRACT)
         stage_w(0, 256, 2, SC)
-        busy(32)
+        busy(16)
         stage_w(1, 256, 2, SC)
-        busy(32)
+        busy(16)
         stage_w(2, 256, 1, VC)
         stage_w(2, 384, 1, SC)
         att_0 = gate(0)

@@ -77,11 +77,11 @@ def tile_parentgru_pb_s_kernel(
         load_x(0)
         load_x(2)
         load_w(2, 0, 2)
-        nc.sync.dma_start(out=c_raw[:], in_=c)
         load_w(0, 256, 2)
         load_w(1, 256, 2)
         load_w(2, 256, 1)
         load_w(2, 384, 1)
+        nc.sync.dma_start(out=c_raw[:], in_=c)
 
         x_codes = keep.tile([P, TERMS, P], U32, align_bytes=64)
         x_scales = keep.tile([P, TERMS, P], U8, align_bytes=64)
@@ -171,7 +171,7 @@ def tile_parentgru_pb_s_kernel(
         stage_x(STATE, VC)
         stage_w(0, 0, 2, SC)
         busy(16)
-        stage_w(1, 0, 2, VC)
+        stage_w(1, 0, 2, SC)
         busy(16)
         for j in range(BLOCKS):
             nc.tensor.matmul(
@@ -183,7 +183,6 @@ def tile_parentgru_pb_s_kernel(
         busy(16)
         stage_w(2, 0, 2, SC)
         busy(16)
-        nc.vector.tensor_tensor(out=diff[:], in0=c_raw[:], in1=x_raw[STATE][:], op=SUBTRACT)
         stage_w(0, 256, 2, SC)
         busy(16)
         stage_w(1, 256, 2, SC)
@@ -193,14 +192,15 @@ def tile_parentgru_pb_s_kernel(
         att_0 = gate(0)
         att_1 = gate(1)
         quantise(*pending.pop())
+        nc.vector.tensor_tensor(out=diff[:], in0=c_raw[:], in1=x_raw[STATE][:], op=SUBTRACT)
         att_2 = gate(2)
         att_3 = gate(3)
         turned_a = turn((att_0, att_1))
         product_a = scale_by_diff(turned_a, cols_a, 256)
         turned_b = turn((att_2,))
         turned_c = turn((att_3,))
-        finish(product_a, cols_a, 256)
         product_b = scale_by_diff(turned_b, cols_b, P)
         product_c = scale_by_diff(turned_c, cols_c, P)
+        finish(product_a, cols_a, 256)
         finish(product_b, cols_b, P)
         finish(product_c, cols_c, P)

@@ -19,8 +19,8 @@ HID = 512
 BLOCKS = HID // P
 TERMS = 3
 STATE = 1
-HALVES = 2
-WARM_UPS = 4
+WORDS = 2
+WARM_UPS = 3
 
 FLOPS = 2 * P * K * HID * TERMS
 
@@ -36,22 +36,20 @@ def tile_parentgru_pb_s_kernel(
     with ExitStack() as ctx:
         keep = ctx.enter_context(tc.tile_pool(name="keep", bufs=1))
         work = ctx.enter_context(tc.tile_pool(name="work", bufs=4))
-        psum_t = ctx.enter_context(tc.psum_pool(name="psum_t", bufs=4))
-        psum_acc = ctx.enter_context(tc.psum_pool(name="psum_acc", bufs=2))
-        psum_idle = ctx.enter_context(tc.psum_pool(name="psum_idle", bufs=1))
-        psum_bias = ctx.enter_context(tc.psum_pool(name="psum_bias", bufs=1))
+        psum_t = ctx.enter_context(tc.psum_pool(name="psum_t", bufs=5))
+        psum_acc = ctx.enter_context(tc.psum_pool(name="psum_acc", bufs=3))
         ctx.enter_context(tc.manual_schedule())
 
         warm_src = keep.tile([P, P], F32)
         nc.vector.memset(warm_src[:], 1.0)
         ident = keep.tile([P, P], F32)
         make_identity(nc, ident[:])
+        bias_row = keep.tile([P, HID], BF16)
+        nc.vector.memset(bias_row[:].bitcast(F32), 0.0)
         warm_in = keep.tile([P, 1], F32)
         nc.vector.memset(warm_in[:], 0.0)
         warm_out = keep.tile([P, 1], F32)
         nc.scalar.activation(out=warm_out[:], in_=warm_in[:], func=SIGMOID)
-        bias_row = keep.tile([P, HID], BF16)
-        nc.vector.memset(bias_row[:], 0.0)
         ones = keep.tile([P, 1], BF16)
         nc.vector.memset(ones[:], 1.0)
 
@@ -62,72 +60,70 @@ def tile_parentgru_pb_s_kernel(
         def load_x(a):
             nc.sync.dma_start(out=x_raw[a][:], in_=acts[a])
 
-        def load_w(a, first, blocks):
-            raw = keep.tile([P, blocks * K], BF16, name="w_raw%d_%d" % (a, first))
-            nc.sync.dma_start(
-                out=raw[:],
-                in_=weights[a][first : first + blocks * P, :].rearrange("(p t) k -> p (t k)", t=blocks),
-            )
-            w_raw[(a, first)] = raw
+        def load_w(a, half):
+            raw = keep.tile([P, 2, K], BF16, name="w_raw%d_%d" % (a, half))
+            rows = weights[a][half * 2 * P : (half + 1) * 2 * P, :]
+            nc.sync.dma_start(out=raw[:], in_=rows.rearrange("(p t) k -> p t k", t=2))
+            for t in range(2):
+                w_raw[(a, half, t)] = raw[:, t, :]
+
+        def load_w_rows(a, half, t):
+            raw = keep.tile([P, K], BF16, name="w_raw%d_%d_%d" % (a, half, t))
+            rows = weights[a][half * 2 * P : (half + 1) * 2 * P, :]
+            nc.sync.dma_start(out=raw[:], in_=rows.rearrange("(p t) k -> p t k", t=2)[:, t, :])
+            w_raw[(a, half, t)] = raw[:]
 
         load_x(STATE)
-        load_w(0, 0, 2)
-        load_w(1, 0, 2)
+        load_w(0, 0)
+        load_w(1, 0)
         nc.sync.dma_start(out=bias_row[0:1, :], in_=w_a_b.rearrange("(o h) -> o h", o=1))
         load_x(0)
         load_x(2)
-        load_w(2, 0, 2)
-        load_w(0, 256, 2)
-        load_w(1, 256, 2)
-        load_w(2, 256, 1)
-        load_w(2, 384, 1)
+        load_w(2, 0)
+        load_w(0, 1)
+        load_w(1, 1)
+        load_w_rows(2, 1, 0)
+        load_w_rows(2, 1, 1)
         nc.sync.dma_start(out=c_raw[:], in_=c)
 
         x_codes = keep.tile([P, TERMS, P], U32, align_bytes=64)
         x_scales = keep.tile([P, TERMS, P], U8, align_bytes=64)
-        w_codes = keep.tile([P, TERMS, HID], U32, align_bytes=64)
-        w_scales = keep.tile([P, TERMS, HID], U8, align_bytes=64)
-
-        def transpose_rows(raw, blocks, copy):
-            words = raw[:].bitcast(F32)
-            bank = psum_t.tile([P, blocks, HALVES, P], F32, tag="bank")
-            for t in range(blocks):
-                for u in range(HALVES):
-                    first_word = (t * HALVES + u) * P
-                    nc.tensor.transpose(bank[:, t, u, :], words[:, first_word : first_word + P], ident[:])
-            grouped = work.tile([P, blocks * K], BF16, align_bytes=64, tag="grouped%d" % blocks)
-            copy(
-                out=grouped[:].bitcast(F32).rearrange("p (j t u) -> p j t u", t=blocks, u=HALVES),
-                in_=bank[:].rearrange("p t u j -> p j t u"),
-            )
-            return grouped
+        w_codes = keep.tile([P, TERMS, BLOCKS, P], U32, align_bytes=64)
+        w_scales = keep.tile([P, TERMS, BLOCKS, P], U8, align_bytes=64)
 
         def quantise(grouped, codes, scales):
             nc.vector.quantize_mx(out=codes.bitcast(FP8X4), scales=scales, in_=grouped[:])
 
         pending = []
 
-        def stage(raw, blocks, copy, codes, scales):
-            grouped = transpose_rows(raw, blocks, copy)
+        def stage(rows, copy, codes, scales):
+            words = rows.bitcast(F32)
+            bank = psum_t.tile([P, WORDS, P], F32, tag="bank")
+            for u in range(WORDS):
+                nc.tensor.transpose(bank[:, u, :], words[:, u * P : (u + 1) * P], ident[:])
+            grouped = work.tile([P, K], BF16, align_bytes=64, tag="grouped")
+            copy(
+                out=grouped[:].bitcast(F32).rearrange("p (j u) -> p j u", u=WORDS),
+                in_=bank[:].rearrange("p u j -> p j u"),
+            )
             if pending:
                 quantise(*pending.pop())
             pending.append((grouped, codes, scales))
 
         def stage_x(a, copy):
-            stage(x_raw[a], 1, copy, x_codes[:, a, :], x_scales[:, a, :])
+            stage(x_raw[a][:], copy, x_codes[:, a, :], x_scales[:, a, :])
 
-        def stage_w(a, first, blocks, copy):
-            cols = slice(first, first + blocks * P)
-            stage(w_raw[(a, first)], blocks, copy, w_codes[:, a, cols], w_scales[:, a, cols])
+        def stage_w(a, half, t, copy):
+            block = half * 2 + t
+            stage(w_raw[(a, half, t)], copy, w_codes[:, a, block, :], w_scales[:, a, block, :])
 
         def gate(block):
-            cols = slice(block * P, (block + 1) * P)
             acc = psum_acc.tile([P, P], F32, tag="acc")
             for a in range(TERMS):
                 nc.tensor.matmul_mx(
                     out=acc[:],
-                    lhsT=w_codes[:, a, cols].bitcast(FP8X4),
-                    lhsT_scale=w_scales[:, a, cols],
+                    lhsT=w_codes[:, a, block, :].bitcast(FP8X4),
+                    lhsT_scale=w_scales[:, a, block, :],
                     rhs=x_codes[:, a, :].bitcast(FP8X4),
                     rhs_scale=x_scales[:, a, :],
                     start=(a == 0),
@@ -143,64 +139,64 @@ def tile_parentgru_pb_s_kernel(
                 nc.tensor.transpose(bank[:, i, :], att[:], ident[:])
             return bank
 
-        def scale_by_diff(bank, cols, width):
-            product = work.tile([P, width], F32, tag="moved")
-            nc.vector.tensor_tensor(
-                out=product[:], in0=bank[:].rearrange("p i h -> p (i h)"), in1=diff[:, cols], op=MULT
-            )
-            return product
+        def scale_by_diff(out, bank, diff_cols):
+            nc.vector.tensor_tensor(out=out, in0=bank, in1=diff_cols, op=MULT)
 
-        def finish(product, cols, width):
-            result = work.tile([P, width], F32, tag="result")
-            nc.vector.tensor_tensor(out=result[:], in0=product[:], in1=x_raw[STATE][:, cols], op=ADD)
+        def finish(product, half):
+            cols = slice(half * 2 * P, (half + 1) * 2 * P)
+            result = work.tile([P, 2 * P], F32, tag="result")
+            nc.vector.tensor_tensor(
+                out=result[:].rearrange("p (j t) -> p j t", t=2),
+                in0=product[:].rearrange("p t j -> p j t"),
+                in1=x_raw[STATE][:, cols].rearrange("p (j t) -> p j t", t=2),
+                op=ADD,
+            )
             nc.sync.dma_start(out=out[:, cols], in_=result[:])
 
-        def busy(width):
-            nc.tensor.matmul(idle_ps[:, 0:width], lhsT=warm_src[:], rhs=warm_src[:, 0:width], start=True, stop=True)
-
-        cols_a, cols_b, cols_c = slice(0, 256), slice(256, 384), slice(384, 512)
-        diff = keep.tile([P, HID], F32)
-        bias_ps = psum_bias.tile([P, HID], F32)
-        idle_ps = psum_idle.tile([P, P], F32)
+        diff = [keep.tile([P, 2 * P], F32, name="diff%d" % half) for half in range(2)]
+        diff_blocks = [d[:].rearrange("p (j t) -> p t j", t=2) for d in diff]
+        idle_ps = psum_acc.tile([P, P], F32, tag="acc")
         bias_col = keep.tile([P, BLOCKS], F32)
 
         for i in range(WARM_UPS):
-            busy(P)
-        for i in range(4):
-            nc.tensor.transpose(idle_ps[:], ident[:], ident[:])
+            nc.tensor.matmul(idle_ps[:], lhsT=warm_src[:], rhs=warm_src[:], start=True, stop=True)
         stage_x(STATE, VC)
-        stage_w(0, 0, 2, SC)
-        busy(16)
-        stage_w(1, 0, 2, SC)
-        busy(16)
+        stage_w(0, 0, 0, SC)
+        stage_w(0, 0, 1, VC)
+        stage_w(1, 0, 0, SC)
+        stage_w(1, 0, 1, VC)
+        bias_ps = psum_t.tile([P, BLOCKS], F32, tag="bank")
         for j in range(BLOCKS):
+            first = (j // 2) * 2 * P + j % 2
             nc.tensor.matmul(
-                bias_ps[:, j : j + 1], lhsT=bias_row[:, j * P : (j + 1) * P], rhs=ones[:], start=True, stop=True
+                bias_ps[:, j : j + 1], lhsT=bias_row[:, first : first + 2 * P - 1 : 2], rhs=ones[:], start=True, stop=True
             )
         stage_x(0, SC)
-        nc.scalar.copy(out=bias_col[:], in_=bias_ps[:, 0:BLOCKS])
+        nc.scalar.copy(out=bias_col[:], in_=bias_ps[:])
         stage_x(2, SC)
-        busy(16)
-        stage_w(2, 0, 2, SC)
-        busy(16)
-        stage_w(0, 256, 2, SC)
-        busy(16)
-        stage_w(1, 256, 2, SC)
-        busy(16)
-        stage_w(2, 256, 1, VC)
-        stage_w(2, 384, 1, SC)
+        stage_w(2, 0, 0, SC)
+        stage_w(2, 0, 1, SC)
+        stage_w(0, 1, 0, SC)
+        stage_w(0, 1, 1, SC)
+        stage_w(1, 1, 0, SC)
+        stage_w(1, 1, 1, VC)
+        stage_w(2, 1, 0, SC)
+        stage_w(2, 1, 1, SC)
         att_0 = gate(0)
         att_1 = gate(1)
         quantise(*pending.pop())
-        nc.vector.tensor_tensor(out=diff[:], in0=c_raw[:], in1=x_raw[STATE][:], op=SUBTRACT)
+        for half in range(2):
+            cols = slice(half * 2 * P, (half + 1) * 2 * P)
+            nc.vector.tensor_tensor(out=diff[half][:], in0=c_raw[:, cols], in1=x_raw[STATE][:, cols], op=SUBTRACT)
         att_2 = gate(2)
         att_3 = gate(3)
         turned_a = turn((att_0, att_1))
-        product_a = scale_by_diff(turned_a, cols_a, 256)
+        product_a = work.tile([P, 2, P], F32, tag="product")
+        scale_by_diff(product_a[:], turned_a[:], diff_blocks[0])
         turned_b = turn((att_2,))
         turned_c = turn((att_3,))
-        product_b = scale_by_diff(turned_b, cols_b, P)
-        product_c = scale_by_diff(turned_c, cols_c, P)
-        finish(product_a, cols_a, 256)
-        finish(product_b, cols_b, P)
-        finish(product_c, cols_c, P)
+        product_b = work.tile([P, 2, P], F32, tag="product")
+        scale_by_diff(product_b[:, 0, :], turned_b[:, 0, :], diff_blocks[1][:, 0, :])
+        scale_by_diff(product_b[:, 1, :], turned_c[:, 0, :], diff_blocks[1][:, 1, :])
+        finish(product_a, 0)
+        finish(product_b, 1)

@@ -20,7 +20,7 @@ BLOCKS = HID // P
 TERMS = 3
 STATE = 1
 WORDS = 2
-WARM_UPS = 3
+WARM_UPS = 4
 
 FLOPS = 2 * P * K * HID * TERMS
 
@@ -142,16 +142,21 @@ def tile_parentgru_pb_s_kernel(
         def scale_by_diff(out, bank, diff_cols):
             nc.vector.tensor_tensor(out=out, in0=bank, in1=diff_cols, op=MULT)
 
-        def finish(product, half):
-            cols = slice(half * 2 * P, (half + 1) * 2 * P)
-            result = work.tile([P, 2 * P], F32, tag="result")
-            nc.vector.tensor_tensor(
-                out=result[:].rearrange("p (j t) -> p j t", t=2),
-                in0=product[:].rearrange("p t j -> p j t"),
-                in1=x_raw[STATE][:, cols].rearrange("p (j t) -> p j t", t=2),
-                op=ADD,
-            )
-            nc.sync.dma_start(out=out[:, cols], in_=result[:])
+        def finish(product, half, pieces):
+            width = 2 * P // pieces
+            for i in range(pieces):
+                cols = slice(half * 2 * P + i * width, half * 2 * P + (i + 1) * width)
+                result = work.tile([P, width], F32, tag="result")
+                nc.vector.tensor_tensor(
+                    out=result[:].rearrange("p (j t) -> p j t", t=2),
+                    in0=product[:, :, i * width // 2 : (i + 1) * width // 2].rearrange("p t j -> p j t"),
+                    in1=x_raw[STATE][:, cols].rearrange("p (j t) -> p j t", t=2),
+                    op=ADD,
+                )
+                nc.sync.dma_start(out=out[:, cols], in_=result[:])
+
+        def busy(width):
+            nc.tensor.matmul(idle_ps[:, 0:width], lhsT=warm_src[:], rhs=warm_src[:, 0:width], start=True, stop=True)
 
         diff = [keep.tile([P, 2 * P], F32, name="diff%d" % half) for half in range(2)]
         diff_blocks = [d[:].rearrange("p (j t) -> p t j", t=2) for d in diff]
@@ -159,12 +164,14 @@ def tile_parentgru_pb_s_kernel(
         bias_col = keep.tile([P, BLOCKS], F32)
 
         for i in range(WARM_UPS):
-            nc.tensor.matmul(idle_ps[:], lhsT=warm_src[:], rhs=warm_src[:], start=True, stop=True)
+            busy(P)
         stage_x(STATE, VC)
         stage_w(0, 0, 0, SC)
         stage_w(0, 0, 1, VC)
+        busy(16)
         stage_w(1, 0, 0, SC)
         stage_w(1, 0, 1, VC)
+        busy(16)
         bias_ps = psum_t.tile([P, BLOCKS], F32, tag="bank")
         for j in range(BLOCKS):
             first = (j // 2) * 2 * P + j % 2
@@ -174,12 +181,16 @@ def tile_parentgru_pb_s_kernel(
         stage_x(0, SC)
         nc.scalar.copy(out=bias_col[:], in_=bias_ps[:])
         stage_x(2, SC)
+        busy(16)
         stage_w(2, 0, 0, SC)
         stage_w(2, 0, 1, SC)
+        busy(16)
         stage_w(0, 1, 0, SC)
         stage_w(0, 1, 1, SC)
+        busy(16)
         stage_w(1, 1, 0, SC)
         stage_w(1, 1, 1, VC)
+        busy(16)
         stage_w(2, 1, 0, SC)
         stage_w(2, 1, 1, SC)
         att_0 = gate(0)
@@ -198,5 +209,5 @@ def tile_parentgru_pb_s_kernel(
         product_b = work.tile([P, 2, P], F32, tag="product")
         scale_by_diff(product_b[:, 0, :], turned_b[:, 0, :], diff_blocks[1][:, 0, :])
         scale_by_diff(product_b[:, 1, :], turned_c[:, 0, :], diff_blocks[1][:, 1, :])
-        finish(product_a, 0)
-        finish(product_b, 1)
+        finish(product_a, 0, 1)
+        finish(product_b, 1, 2)

from contextlib import ExitStack

import concourse.mybir as mybir
from concourse.masks import make_identity

F32 = mybir.dt.float32
BF16 = mybir.dt.bfloat16
U32 = mybir.dt.uint32
U8 = mybir.dt.uint8
FP8X4 = mybir.dt.float8_e4m3fn_x4
ADD = mybir.AluOpType.add
SUBTRACT = mybir.AluOpType.subtract
MULT = mybir.AluOpType.mult
SIGMOID = mybir.ActivationFunctionType.Sigmoid

P = 128
K = 512
HID = 512
BLOCKS = HID // P
TERMS = 3
STATE = 1
WORDS = 2
WARM_UPS = 4

FLOPS = 2 * P * K * HID * TERMS


def tile_parentgru_pb_s_kernel(
    tc, inputs, state, parent_state, c, w_a_w, w_a_b, u_a_w, p_a_w, out
):
    nc = tc.nc
    acts = (inputs, state, parent_state)
    weights = (w_a_w, u_a_w, p_a_w)
    SC, VC = nc.scalar.copy, nc.vector.tensor_copy

    with ExitStack() as ctx:
        keep = ctx.enter_context(tc.tile_pool(name="keep", bufs=1))
        work = ctx.enter_context(tc.tile_pool(name="work", bufs=4))
        psum_t = ctx.enter_context(tc.psum_pool(name="psum_t", bufs=5))
        psum_acc = ctx.enter_context(tc.psum_pool(name="psum_acc", bufs=3))
        ctx.enter_context(tc.manual_schedule())

        warm_src = keep.tile([P, P], F32)
        nc.vector.memset(warm_src[:], 1.0)
        ident = keep.tile([P, P], F32)
        make_identity(nc, ident[:])
        bias_row = keep.tile([P, HID], BF16)
        nc.vector.memset(bias_row[:].bitcast(F32), 0.0)
        warm_in = keep.tile([P, 1], F32)
        nc.vector.memset(warm_in[:], 0.0)
        warm_out = keep.tile([P, 1], F32)
        nc.scalar.activation(out=warm_out[:], in_=warm_in[:], func=SIGMOID)
        ones = keep.tile([P, 1], BF16)
        nc.vector.memset(ones[:], 1.0)

        x_raw = [keep.tile([P, K], BF16, name="x_raw%d" % a) for a in range(TERMS)]
        c_raw = keep.tile([P, HID], BF16)
        w_raw = {}

        def load_x(a):
            nc.sync.dma_start(out=x_raw[a][:], in_=acts[a])

        def load_w(a, half):
            raw = keep.tile([P, 2, K], BF16, name="w_raw%d_%d" % (a, half))
            rows = weights[a][half * 2 * P : (half + 1) * 2 * P, :]
            nc.sync.dma_start(out=raw[:], in_=rows.rearrange("(p t) k -> p t k", t=2))
            for t in range(2):
                w_raw[(a, half, t)] = raw[:, t, :]

        def load_w_rows(a, half, t):
            raw = keep.tile([P, K], BF16, name="w_raw%d_%d_%d" % (a, half, t))
            rows = weights[a][half * 2 * P : (half + 1) * 2 * P, :]
            nc.sync.dma_start(out=raw[:], in_=rows.rearrange("(p t) k -> p t k", t=2)[:, t, :])
            w_raw[(a, half, t)] = raw[:]

        load_x(STATE)
        load_w(0, 0)
        load_w(1, 0)
        nc.sync.dma_start(out=bias_row[0:1, :], in_=w_a_b.rearrange("(o h) -> o h", o=1))
        load_x(0)
        load_x(2)
        load_w(2, 0)
        load_w(0, 1)
        load_w(1, 1)
        load_w_rows(2, 1, 0)
        load_w_rows(2, 1, 1)
        nc.sync.dma_start(out=c_raw[:], in_=c)

        x_codes = keep.tile([P, TERMS, P], U32, align_bytes=64)
        x_scales = keep.tile([P, TERMS, P], U8, align_bytes=64)
        w_codes = keep.tile([P, TERMS, BLOCKS, P], U32, align_bytes=64)
        w_scales = keep.tile([P, TERMS, BLOCKS, P], U8, align_bytes=64)

        def quantise(grouped, codes, scales):
            nc.vector.quantize_mx(out=codes.bitcast(FP8X4), scales=scales, in_=grouped[:])

        pending = []

        def stage(rows, copy, codes, scales):
            words = rows.bitcast(F32)
            bank = psum_t.tile([P, WORDS, P], F32, tag="bank")
            for u in range(WORDS):
                nc.tensor.transpose(bank[:, u, :], words[:, u * P : (u + 1) * P], ident[:])
            grouped = work.tile([P, K], BF16, align_bytes=64, tag="grouped")
            copy(
                out=grouped[:].bitcast(F32).rearrange("p (j u) -> p j u", u=WORDS),
                in_=bank[:].rearrange("p u j -> p j u"),
            )
            if pending:
                quantise(*pending.pop())
            pending.append((grouped, codes, scales))

        def stage_x(a, copy):
            stage(x_raw[a][:], copy, x_codes[:, a, :], x_scales[:, a, :])

        def stage_w(a, half, t, copy):
            block = half * 2 + t
            stage(w_raw[(a, half, t)], copy, w_codes[:, a, block, :], w_scales[:, a, block, :])

        def gate(block):
            acc = psum_acc.tile([P, P], F32, tag="acc")
            for a in range(TERMS):
                nc.tensor.matmul_mx(
                    out=acc[:],
                    lhsT=w_codes[:, a, block, :].bitcast(FP8X4),
                    lhsT_scale=w_scales[:, a, block, :],
                    rhs=x_codes[:, a, :].bitcast(FP8X4),
                    rhs_scale=x_scales[:, a, :],
                    start=(a == 0),
                    stop=(a == TERMS - 1),
                )
            att = work.tile([P, P], F32, tag="att")
            nc.scalar.activation(out=att[:], in_=acc[:], func=SIGMOID, bias=bias_col[:, block : block + 1])
            return att

        def turn(atts):
            bank = psum_t.tile([P, len(atts), P], F32, tag="bank")
            for i, att in enumerate(atts):
                nc.tensor.transpose(bank[:, i, :], att[:], ident[:])
            return bank

        def scale_by_diff(out, bank, diff_cols):
            nc.vector.tensor_tensor(out=out, in0=bank, in1=diff_cols, op=MULT)

        def finish(product, half, pieces):
            width = 2 * P // pieces
            for i in range(pieces):
                cols = slice(half * 2 * P + i * width, half * 2 * P + (i + 1) * width)
                result = work.tile([P, width], F32, tag="result")
                nc.vector.tensor_tensor(
                    out=result[:].rearrange("p (j t) -> p j t", t=2),
                    in0=product[:, :, i * width // 2 : (i + 1) * width // 2].rearrange("p t j -> p j t"),
                    in1=x_raw[STATE][:, cols].rearrange("p (j t) -> p j t", t=2),
                    op=ADD,
                )
                nc.sync.dma_start(out=out[:, cols], in_=result[:])

        def busy(width):
            nc.tensor.matmul(idle_ps[:, 0:width], lhsT=warm_src[:], rhs=warm_src[:, 0:width], start=True, stop=True)

        diff = [keep.tile([P, 2 * P], F32, name="diff%d" % half) for half in range(2)]
        diff_blocks = [d[:].rearrange("p (j t) -> p t j", t=2) for d in diff]
        idle_ps = psum_acc.tile([P, P], F32, tag="acc")
        bias_col = keep.tile([P, BLOCKS], F32)

        for i in range(WARM_UPS):
            busy(P)
        stage_x(STATE, VC)
        stage_w(0, 0, 0, SC)
        stage_w(0, 0, 1, VC)
        busy(16)
        stage_w(1, 0, 0, SC)
        stage_w(1, 0, 1, VC)
        busy(16)
        bias_ps = psum_t.tile([P, BLOCKS], F32, tag="bank")
        for j in range(BLOCKS):
            first = (j // 2) * 2 * P + j % 2
            nc.tensor.matmul(
                bias_ps[:, j : j + 1], lhsT=bias_row[:, first : first + 2 * P - 1 : 2], rhs=ones[:], start=True, stop=True
            )
        stage_x(0, SC)
        nc.scalar.copy(out=bias_col[:], in_=bias_ps[:])
        stage_x(2, SC)
        busy(16)
        stage_w(2, 0, 0, SC)
        stage_w(2, 0, 1, SC)
        busy(16)
        stage_w(0, 1, 0, SC)
        stage_w(0, 1, 1, SC)
        busy(16)
        stage_w(1, 1, 0, SC)
        stage_w(1, 1, 1, VC)
        busy(16)
        stage_w(2, 1, 0, SC)
        stage_w(2, 1, 1, SC)
        att_0 = gate(0)
        att_1 = gate(1)
        quantise(*pending.pop())
        for half in range(2):
            cols = slice(half * 2 * P, (half + 1) * 2 * P)
            nc.vector.tensor_tensor(out=diff[half][:], in0=c_raw[:, cols], in1=x_raw[STATE][:, cols], op=SUBTRACT)
        att_2 = gate(2)
        att_3 = gate(3)
        turned_a = turn((att_0, att_1))
        product_a = work.tile([P, 2, P], F32, tag="product")
        scale_by_diff(product_a[:], turned_a[:], diff_blocks[0])
        turned_b = turn((att_2,))
        turned_c = turn((att_3,))
        product_b = work.tile([P, 2, P], F32, tag="product")
        scale_by_diff(product_b[:, 0, :], turned_b[:, 0, :], diff_blocks[1][:, 0, :])
        scale_by_diff(product_b[:, 1, :], turned_c[:, 0, :], diff_blocks[1][:, 1, :])
        finish(product_a, 0, 1)
        finish(product_b, 1, 2)
